import numpy as np
import ml_dtypes


def mxq(x, axis, fmt="e4m3"):
    dtype, down = {"e4m3": (ml_dtypes.float8_e4m3fn, 7), "e5m2": (ml_dtypes.float8_e5m2, 14)}[fmt]
    v = np.moveaxis(np.asarray(x, np.float32).astype(ml_dtypes.bfloat16).astype(np.float64), axis, -1)
    blocks = v.reshape(v.shape[:-1] + (-1, 32))
    amax = np.abs(blocks).max(-1, keepdims=True)
    byte = np.maximum(np.where(amax > 0, np.frexp(amax)[1] - 1 + 127, 0) - down, 1)
    scale = np.exp2(byte - 127.0)
    codes = (blocks / scale).astype(np.float32).astype(dtype).astype(np.float64)
    return np.moveaxis((codes * scale).reshape(v.shape), -1, axis)


WIDE = False


def mx_kscale(k):
    if not WIDE:
        return np.ones(k)
    levels = np.array([10, -10, 5, -5, 0])
    a = np.random.permutation(np.resize(levels, k // 512 * 4)).reshape(k // 512, 4)
    idx = np.arange(k)
    return np.exp2(a[idx // 512, idx % 128 // 32])


BF16 = ml_dtypes.bfloat16


def bf(x):
    return np.asarray(x, np.float32).astype(BF16)


def f64(x):
    return np.asarray(x).astype(np.float64)


B, S, E, H, KV, HD = 1, 512, 2048, 16, 4, 128
G = H // KV


def setup_inputs():
    t = mx_kscale(H * HD).reshape(KV, G, HD)[:, 0, :]
    v_level = (1.5 + np.random.random((B, KV, HD))) * np.sign(np.random.standard_normal((B, KV, HD)))
    return {
        "q_rot": bf(np.random.standard_normal((B, H, S, HD)) * 1.2),
        "k_rot": bf(np.random.standard_normal((B, KV, S, HD)) * 1.2),
        "v": bf((v_level[:, :, None, :] + np.random.standard_normal((B, KV, S, HD)) * 2.0) * t[None, :, None, :]),
        "wo": bf(np.random.standard_normal((H * HD, E)) / np.sqrt(H * HD) / np.repeat(t, G, axis=0).reshape(H * HD)[:, None]),
    }


def reference(q_rot, k_rot, v, wo):
    s = f64(q_rot).reshape(B, KV, G, S, HD) @ f64(k_rot).transpose(0, 1, 3, 2)[:, :, None] / np.sqrt(HD)
    e = np.exp(s - s.max(-1, keepdims=True))
    vq = mxq(f64(v), 2, "e4m3")[:, :, None]
    y = (mxq(e, 4, "e4m3") @ vq) / e.sum(-1, keepdims=True)
    y = y.reshape(B, H, S, HD).transpose(0, 2, 1, 3).reshape(B, S, H * HD)
    return mxq(y, 2, "e4m3") @ mxq(f64(wo), 0, "e4m3")

@@ -1,0 +1,342 @@
+import math
+from contextlib import ExitStack
+
+import concourse.mybir as mybir
+from concourse.masks import make_identity
+
+F32 = mybir.dt.float32
+BF16 = mybir.dt.bfloat16
+U32 = mybir.dt.uint32
+U8 = mybir.dt.uint8
+FP8X4 = mybir.dt.float8_e4m3fn_x4
+EXP = mybir.ActivationFunctionType.Exp
+COPY = mybir.ActivationFunctionType.Copy
+MAX = mybir.AluOpType.max
+AXIS_X = mybir.AxisListType.X
+
+P = 128
+H, KV, S, HD, E = 16, 4, 512, 128, 2048
+G = H // KV
+QT = S // P
+PACK = 4
+HALF = 2
+N_TILE = 512
+NT = E // N_TILE
+STEPS = H * QT
+UNITS = STEPS // G
+CHUNKS = KV * NT
+SCALE = 1.0 / math.sqrt(HD)
+
+SCORES_AHEAD = 3
+MAX_AHEAD = 2
+BIAS_AHEAD = 1
+AT_Q = -7
+AT_E_QUANT = G + 1
+AT_PV = AT_E_QUANT + 1
+AT_Y_TRANSPOSE = AT_PV + 1
+AT_Y_COPY = AT_Y_TRANSPOSE + 1
+AT_Y_QUANT = AT_Y_COPY + 1
+WO_FIRST = 6
+WO_EVERY = 3
+FIRST_STEP = AT_Q
+LAST_TILES_FIRST = STEPS
+LAST_STEP = LAST_TILES_FIRST + 2 * (KV - 1)
+
+FLOPS = 2 * H * S * S * HD * 2 + 2 * S * (H * HD) * E
+
+
+def unit_at(step, lag):
+    first = step - lag
+    if first % G == 0 and 0 <= first < STEPS:
+        return first // G
+    return -1
+
+
+def tile_grupedqueryattention_pb_kernel(tc, q_rot, k_rot, v, wo, out):
+    nc = tc.nc
+    with ExitStack() as ctx:
+        keep = ctx.enter_context(tc.tile_pool(name="keep", bufs=1))
+        work = ctx.enter_context(tc.tile_pool(name="work", bufs=2))
+        psum_s = ctx.enter_context(tc.psum_pool(name="psum_s", bufs=SCORES_AHEAD + 1))
+        psum_e = ctx.enter_context(tc.psum_pool(name="psum_e", bufs=1))
+        psum_t = ctx.enter_context(tc.psum_pool(name="psum_t", bufs=1))
+        psum_y = ctx.enter_context(tc.psum_pool(name="psum_y", bufs=1))
+        psum_o = ctx.enter_context(tc.psum_pool(name="psum_o", bufs=1))
+        ctx.enter_context(tc.manual_schedule())
+
+        q_view = q_rot[0].rearrange("(g h) (p t) d -> g p h (t d)", h=G, t=QT)
+        out_view = out[0].rearrange("(p t) n -> t p n", t=QT)
+        k_view = k_rot[0].rearrange("g (t p) d -> g p t d", p=P)
+        v_view = v[0].rearrange("g (u p e) d -> p (g u) (e d)", u=HALF, e=2)
+        wo_view = wo.rearrange("(g u p e) n -> e p (g u) n", g=KV, u=HALF, e=2)
+
+        q_raw = [keep.tile([P, G, QT * HD], BF16, name="q_raw%d" % g) for g in range(KV)]
+        k_raw = [keep.tile([P, QT, HD], BF16, name="k_raw%d" % g) for g in range(KV)]
+        k_t = [keep.tile([P, S], BF16, name="k_t%d" % g) for g in range(KV)]
+        v_raw = keep.tile([P, KV, PACK, HD], BF16, name="v_raw")
+        v_grouped = keep.tile([P, KV * HD * PACK], BF16, name="v_grouped", align_bytes=64)
+        v_codes = keep.tile([P, KV * HD], U32, name="v_codes", align_bytes=64)
+        v_scales = keep.tile([P, KV * HD], U8, name="v_scales", align_bytes=64)
+        w_raw = [keep.tile([P, KV, PACK, N_TILE], BF16, name="w_raw%d" % nt) for nt in range(NT)]
+        w_codes = keep.tile([P, KV, E], U32, name="w_codes", align_bytes=64)
+        w_scales = keep.tile([P, KV, E], U8, name="w_scales", align_bytes=64)
+        y_grouped = [
+            keep.tile([P, KV * P * PACK], BF16, name="y_grouped%d" % t, align_bytes=64) for t in range(QT)
+        ]
+        y_codes = [keep.tile([P, KV * P], U32, name="y_codes%d" % t, align_bytes=64) for t in range(QT)]
+        y_scales = [keep.tile([P, KV * P], U8, name="y_scales%d" % t, align_bytes=64) for t in range(QT)]
+        row_max = keep.tile([P, STEPS], F32, name="row_max")
+        exp_bias = keep.tile([P, STEPS], F32, name="exp_bias")
+        row_sum = keep.tile([P, STEPS], F32, name="row_sum")
+        inv_sum = keep.tile([P, STEPS], F32, name="inv_sum")
+        ident_bf = keep.tile([P, P], BF16, name="ident_bf")
+        ident_f32 = keep.tile([P, P], F32, name="ident_f32")
+
+        for g in range(KV):
+            nc.sync.dma_start(out=k_raw[g][:], in_=k_view[g])
+            nc.sync.dma_start(out=q_raw[g][:], in_=q_view[g])
+            if g == 1:
+                nc.sync.dma_start(
+                    out=v_raw[:].rearrange("p g (u e) d -> p (g u) (e d)", u=HALF, e=2), in_=v_view
+                )
+        for nt in range(NT):
+            for e in range(2):
+                nc.sync.dma_start(
+                    out=w_raw[nt][:, :, e::2, :].rearrange("p g u n -> p (g u) n"),
+                    in_=wo_view[e][:, :, nt * N_TILE : (nt + 1) * N_TILE],
+                )
+
+        make_identity(nc, ident_bf[:])
+        make_identity(nc, ident_f32[:])
+
+        q_t, scores, e_rows, bank_e, e_grouped, e_codes, e_scales = {}, {}, {}, {}, {}, {}, {}
+        bank_y, y_rows, bank_yt, w_grouped, acc, last_acc = {}, {}, {}, {}, {}, {}
+
+        def transposed_words(bank, rows_bf16):
+            words = rows_bf16.bitcast(F32)
+            for u in range(HALF):
+                nc.tensor.transpose(bank[:, u, :], words[:, u * P : (u + 1) * P], ident_f32[:])
+
+        def score_matmul(n):
+            unit, h = n // G, n % G
+            scores[n] = psum_s.tile([P, S], F32, name="scores", tag="s")
+            nc.tensor.matmul(
+                out=scores[n][:],
+                lhsT=q_t[unit][:, h * P : (h + 1) * P],
+                rhs=k_t[unit % KV][:],
+                start=True,
+                stop=True,
+            )
+
+        def score_max(n):
+            nc.vector.tensor_reduce(out=row_max[:, n : n + 1], in_=scores[n][:], axis=AXIS_X, op=MAX)
+
+        def score_bias(n):
+            nc.scalar.mul(out=exp_bias[:, n : n + 1], in_=row_max[:, n : n + 1], mul=-SCALE)
+
+        def exponentials(n):
+            e_rows[n] = work.tile([P, S], BF16, name="e_rows", bufs=3)
+            nc.scalar.activation(
+                out=e_rows[n][:],
+                in_=scores[n][:],
+                func=EXP,
+                bias=exp_bias[:, n : n + 1],
+                scale=SCALE,
+                accum_out=row_sum[:, n : n + 1],
+            )
+
+        def e_transpose(n):
+            bank_e[n] = psum_e.tile([P, HALF, P], F32, name="bank_e")
+            transposed_words(bank_e[n][:], e_rows[n][:])
+
+        def e_copy(n):
+            unit, h = n // G, n % G
+            if h == 0:
+                e_grouped[unit] = work.tile([P, G * P * PACK], BF16, name="e_grouped", align_bytes=64)
+            e_words = e_grouped[unit][:].bitcast(F32).rearrange("p (h q u) -> p h q u", h=G, u=HALF)
+            nc.scalar.copy(out=e_words[:, h], in_=bank_e[n][:].rearrange("p u q -> p q u"))
+
+        def key_transpose(g):
+            bank_k = psum_o.tile([P, S], BF16, name="bank_k", tag="o")
+            for t in range(QT):
+                nc.tensor.transpose(bank_k[:, t * P : (t + 1) * P], k_raw[g][:, t, :], ident_bf[:])
+            nc.scalar.copy(out=k_t[g][:], in_=bank_k[:])
+
+        def query_transpose(unit):
+            qt, g = unit // KV, unit % KV
+            bank_q = psum_t.tile([P, G * P], BF16, name="bank_q", tag="t")
+            for h in range(G):
+                nc.tensor.transpose(
+                    bank_q[:, h * P : (h + 1) * P], q_raw[g][:, h, qt * HD : (qt + 1) * HD], ident_bf[:]
+                )
+            q_t[unit] = work.tile([P, G * P], BF16, name="q_t")
+            nc.scalar.copy(out=q_t[unit][:], in_=bank_q[:])
+
+        def e_quantise(unit):
+            e_codes[unit] = work.tile([P, G * P], U32, name="e_codes", align_bytes=64)
+            e_scales[unit] = work.tile([P, G * P], U8, name="e_scales", align_bytes=64)
+            nc.vector.quantize_mx(
+                out=e_codes[unit][:].bitcast(FP8X4), scales=e_scales[unit][:], in_=e_grouped[unit][:]
+            )
+            heads = slice(unit * G, (unit + 1) * G)
+            nc.vector.reciprocal(out=inv_sum[:, heads], in_=row_sum[:, heads])
+
+        def e_times_v(unit):
+            g = unit % KV
+            bank_y[unit] = psum_y.tile([P, G * HD], F32, name="bank_y")
+            for h in range(G):
+                rows = slice(h * P, (h + 1) * P)
+                nc.tensor.matmul_mx(
+                    out=bank_y[unit][:, h * HD : (h + 1) * HD],
+                    lhsT=e_codes[unit][:, rows].bitcast(FP8X4),
+                    lhsT_scale=e_scales[unit][:, rows],
+                    rhs=v_codes[:, g * HD : (g + 1) * HD].bitcast(FP8X4),
+                    rhs_scale=v_scales[:, g * HD : (g + 1) * HD],
+                    start=True,
+                    stop=True,
+                )
+            y_rows[unit] = work.tile([P, G * HD], BF16, name="y_rows")
+            for h in range(G):
+                nc.scalar.activation(
+                    out=y_rows[unit][:, h * HD : (h + 1) * HD],
+                    in_=bank_y[unit][:, h * HD : (h + 1) * HD],
+                    func=COPY,
+                    scale=inv_sum[:, unit * G + h : unit * G + h + 1],
+                )
+
+        def y_transpose(unit):
+            bank_yt[unit] = psum_t.tile([P, HALF, P], F32, name="bank_yt", tag="t")
+            transposed_words(bank_yt[unit][:], y_rows[unit][:])
+
+        def y_copy(unit):
+            qt, g = unit // KV, unit % KV
+            y_words = y_grouped[qt][:].bitcast(F32).rearrange("p (g q u) -> p g q u", g=KV, u=HALF)
+            nc.scalar.copy(out=y_words[:, g], in_=bank_yt[unit][:].rearrange("p u q -> p q u"))
+
+        def y_quantise(unit):
+            qt, g = unit // KV, unit % KV
+            nc.vector.quantize_mx(
+                out=y_codes[qt][:, g * P : (g + 1) * P].bitcast(FP8X4),
+                scales=y_scales[qt][:, g * P : (g + 1) * P],
+                in_=y_grouped[qt][:, g * P * PACK : (g + 1) * P * PACK],
+            )
+
+        def prepare_v():
+            nc.vector.tensor_copy(
+                out=v_grouped[:].rearrange("p (g d t) -> p g d t", g=KV, t=PACK),
+                in_=v_raw[:].rearrange("p g t d -> p g d t"),
+            )
+            nc.vector.quantize_mx(out=v_codes[:].bitcast(FP8X4), scales=v_scales[:], in_=v_grouped[:])
+
+        def wo_regroup(chunk):
+            nt, g = chunk // KV, chunk % KV
+            w_grouped[chunk] = work.tile([P, N_TILE * PACK], BF16, name="w_grouped", align_bytes=64)
+            nc.vector.tensor_copy(
+                out=w_grouped[chunk][:].rearrange("p (c i t) -> p c t i", i=4, t=PACK),
+                in_=w_raw[nt][:, g].rearrange("p t (c i) -> p c t i", i=4),
+            )
+
+        def wo_quantise(chunk):
+            nt, g = chunk // KV, chunk % KV
+            cols = slice(nt * N_TILE, (nt + 1) * N_TILE)
+            nc.vector.quantize_mx(
+                out=w_codes[:, g, cols].bitcast(FP8X4), scales=w_scales[:, g, cols], in_=w_grouped[chunk][:]
+            )
+
+        def projection_pass(bank, qt, nt, g):
+            rows = slice(g * P, (g + 1) * P)
+            cols = slice(nt * N_TILE, (nt + 1) * N_TILE)
+            nc.tensor.matmul_mx(
+                out=bank[:],
+                lhsT=y_codes[qt][:, rows].bitcast(FP8X4),
+                lhsT_scale=y_scales[qt][:, rows],
+                rhs=w_codes[:, g, cols].bitcast(FP8X4),
+                rhs_scale=w_scales[:, g, cols],
+                start=(g == 0),
+                stop=(g == KV - 1),
+            )
+
+        def store_tile(bank, qt, nt, on_vector):
+            result = work.tile([P, N_TILE], F32, name="result", bufs=4)
+            if on_vector:
+                nc.vector.tensor_copy(out=result[:], in_=bank[:])
+            else:
+                nc.scalar.copy(out=result[:], in_=bank[:])
+            nc.sync.dma_start(out=out_view[qt][:, nt * N_TILE : (nt + 1) * N_TILE], in_=result[:])
+
+        units_ready = 0
+        chunks_ready = 0
+        issued = []
+        stored = 0
+        for step in range(FIRST_STEP, LAST_STEP + 1):
+            if 0 <= step + SCORES_AHEAD < STEPS:
+                score_matmul(step + SCORES_AHEAD)
+            if 0 <= step - 1 < STEPS:
+                e_transpose(step - 1)
+            if 0 <= step + MAX_AHEAD < STEPS:
+                score_max(step + MAX_AHEAD)
+            if 0 <= step + BIAS_AHEAD < STEPS:
+                score_bias(step + BIAS_AHEAD)
+            if 0 <= step < STEPS:
+                exponentials(step)
+            if 0 <= step - 1 < STEPS:
+                e_copy(step - 1)
+
+            unit = unit_at(step, AT_Y_COPY)
+            if unit >= 0:
+                y_copy(unit)
+            unit = unit_at(step, AT_Q)
+            if unit >= 0:
+                if unit < KV:
+                    key_transpose(unit)
+                query_transpose(unit)
+            unit = unit_at(step, AT_E_QUANT)
+            if unit >= 0:
+                e_quantise(unit)
+            unit = unit_at(step, AT_PV)
+            if unit >= 0:
+                e_times_v(unit)
+            unit = unit_at(step, AT_Y_TRANSPOSE)
+            if unit >= 0:
+                y_transpose(unit)
+            unit = unit_at(step, AT_Y_QUANT)
+            if unit >= 0:
+                y_quantise(unit)
+                units_ready = unit + 1
+            if step == 1:
+                prepare_v()
+
+            since = step - WO_FIRST
+            if since >= 0 and since % WO_EVERY == 0 and since // WO_EVERY < CHUNKS:
+                wo_regroup(since // WO_EVERY)
+            if since >= 1 and (since - 1) % WO_EVERY == 0 and (since - 1) // WO_EVERY < CHUNKS:
+                wo_quantise((since - 1) // WO_EVERY)
+                chunks_ready = (since - 1) // WO_EVERY + 1
+
+            if stored < len(issued):
+                qt, nt = issued[stored]
+                store_tile(acc[(qt, nt)], qt, nt, chunks_ready == CHUNKS)
+                stored += 1
+            if step % 2 == 0:
+                ready = [
+                    (qt, nt)
+                    for qt in range(QT - 1)
+                    for nt in range(NT)
+                    if (qt, nt) not in issued and units_ready >= (qt + 1) * KV and chunks_ready >= (nt + 1) * KV
+                ]
+                if ready:
+                    qt, nt = ready[0]
+                    acc[(qt, nt)] = psum_o.tile([P, N_TILE], F32, name="acc", tag="o")
+                    for g in range(KV):
+                        projection_pass(acc[(qt, nt)], qt, nt, g)
+                    issued.append((qt, nt))
+            since = step - LAST_TILES_FIRST
+            if since >= 0 and since % 2 == 0:
+                g = since // 2
+                for nt in range(NT):
+                    if g == 0:
+                        last_acc[nt] = psum_s.tile([P, N_TILE], F32, name="last_acc", tag="s")
+                    projection_pass(last_acc[nt], QT - 1, nt, g)
+        assert len(issued) == (QT - 1) * NT and stored == len(issued)
+        for nt in range(NT):
+            store_tile(last_acc[nt], QT - 1, nt, nt % 2 == 0)

@@ -58,9 +58,8 @@ def tile_grupedqueryattention_pb_kernel(tc, q_rot, k_rot, v, wo, out):
         keep = ctx.enter_context(tc.tile_pool(name="keep", bufs=1))
         work = ctx.enter_context(tc.tile_pool(name="work", bufs=2))
         psum_s = ctx.enter_context(tc.psum_pool(name="psum_s", bufs=SCORES_AHEAD + 1))
-        psum_e = ctx.enter_context(tc.psum_pool(name="psum_e", bufs=1))
+        psum_e = ctx.enter_context(tc.psum_pool(name="psum_e", bufs=2))
         psum_t = ctx.enter_context(tc.psum_pool(name="psum_t", bufs=1))
-        psum_y = ctx.enter_context(tc.psum_pool(name="psum_y", bufs=1))
         psum_o = ctx.enter_context(tc.psum_pool(name="psum_o", bufs=1))
         ctx.enter_context(tc.manual_schedule())
 
@@ -92,7 +91,10 @@ def tile_grupedqueryattention_pb_kernel(tc, q_rot, k_rot, v, wo, out):
         ident_bf = keep.tile([P, P], BF16, name="ident_bf")
         ident_f32 = keep.tile([P, P], F32, name="ident_f32")
 
-        for g in range(KV):
+        nc.sync.dma_start(out=q_raw[0][:, :, :HD], in_=q_view[0][:, :, :HD])
+        nc.sync.dma_start(out=k_raw[0][:], in_=k_view[0])
+        nc.sync.dma_start(out=q_raw[0][:, :, HD:], in_=q_view[0][:, :, HD:])
+        for g in range(1, KV):
             nc.sync.dma_start(out=k_raw[g][:], in_=k_view[g])
             nc.sync.dma_start(out=q_raw[g][:], in_=q_view[g])
             if g == 1:
@@ -183,7 +185,7 @@ def tile_grupedqueryattention_pb_kernel(tc, q_rot, k_rot, v, wo, out):
 
         def e_times_v(unit):
             g = unit % KV
-            bank_y[unit] = psum_y.tile([P, G * HD], F32, name="bank_y")
+            bank_y[unit] = psum_t.tile([P, G * HD], F32, name="bank_y", tag="t")
             for h in range(G):
                 rows = slice(h * P, (h + 1) * P)
                 nc.tensor.matmul_mx(
@@ -228,12 +230,16 @@ def tile_grupedqueryattention_pb_kernel(tc, q_rot, k_rot, v, wo, out):
             )
             nc.vector.quantize_mx(out=v_codes[:].bitcast(FP8X4), scales=v_scales[:], in_=v_grouped[:])
 
-        def wo_regroup(chunk):
+        def wo_regroup(chunk, half):
             nt, g = chunk // KV, chunk % KV
-            w_grouped[chunk] = work.tile([P, N_TILE * PACK], BF16, name="w_grouped", align_bytes=64)
+            if half == 0:
+                w_grouped[chunk] = work.tile([P, N_TILE * PACK], BF16, name="w_grouped", align_bytes=64)
+            cols = slice(half * (N_TILE // 2), (half + 1) * (N_TILE // 2))
             nc.vector.tensor_copy(
-                out=w_grouped[chunk][:].rearrange("p (c i t) -> p c t i", i=4, t=PACK),
-                in_=w_raw[nt][:, g].rearrange("p t (c i) -> p c t i", i=4),
+                out=w_grouped[chunk][:].rearrange("p (n t) -> p n t", t=PACK)[:, cols].rearrange(
+                    "p (c i) t -> p c t i", i=4
+                ),
+                in_=w_raw[nt][:, g, :, cols].rearrange("p t (c i) -> p c t i", i=4),
             )
 
         def wo_quantise(chunk):
@@ -275,10 +281,10 @@ def tile_grupedqueryattention_pb_kernel(tc, q_rot, k_rot, v, wo, out):
                 e_transpose(step - 1)
             if 0 <= step + MAX_AHEAD < STEPS:
                 score_max(step + MAX_AHEAD)
-            if 0 <= step + BIAS_AHEAD < STEPS:
-                score_bias(step + BIAS_AHEAD)
             if 0 <= step < STEPS:
                 exponentials(step)
+            if 0 <= step + BIAS_AHEAD < STEPS:
+                score_bias(step + BIAS_AHEAD)
             if 0 <= step - 1 < STEPS:
                 e_copy(step - 1)
 
@@ -307,11 +313,12 @@ def tile_grupedqueryattention_pb_kernel(tc, q_rot, k_rot, v, wo, out):
                 prepare_v()
 
             since = step - WO_FIRST
-            if since >= 0 and since % WO_EVERY == 0 and since // WO_EVERY < CHUNKS:
-                wo_regroup(since // WO_EVERY)
-            if since >= 1 and (since - 1) % WO_EVERY == 0 and (since - 1) // WO_EVERY < CHUNKS:
-                wo_quantise((since - 1) // WO_EVERY)
-                chunks_ready = (since - 1) // WO_EVERY + 1
+            if 0 <= since < CHUNKS * WO_EVERY:
+                if since % WO_EVERY < 2:
+                    wo_regroup(since // WO_EVERY, since % WO_EVERY)
+                else:
+                    wo_quantise(since // WO_EVERY)
+                    chunks_ready = since // WO_EVERY + 1
 
             if stored < len(issued):
                 qt, nt = issued[stored]

import math
from contextlib import ExitStack

import concourse.mybir as mybir
from concourse.masks import make_identity

F32 = mybir.dt.float32
BF16 = mybir.dt.bfloat16
U32 = mybir.dt.uint32
U8 = mybir.dt.uint8
FP8X4 = mybir.dt.float8_e4m3fn_x4
EXP = mybir.ActivationFunctionType.Exp
COPY = mybir.ActivationFunctionType.Copy
MAX = mybir.AluOpType.max
AXIS_X = mybir.AxisListType.X

P = 128
H, KV, S, HD, E = 16, 4, 512, 128, 2048
G = H // KV
QT = S // P
PACK = 4
HALF = 2
N_TILE = 512
NT = E // N_TILE
STEPS = H * QT
UNITS = STEPS // G
CHUNKS = KV * NT
SCALE = 1.0 / math.sqrt(HD)

SCORES_AHEAD = 3
MAX_AHEAD = 2
BIAS_AHEAD = 1
AT_Q = -7
AT_E_QUANT = G + 1
AT_PV = AT_E_QUANT + 1
AT_Y_TRANSPOSE = AT_PV + 1
AT_Y_COPY = AT_Y_TRANSPOSE + 1
AT_Y_QUANT = AT_Y_COPY + 1
WO_FIRST = 6
WO_EVERY = 3
FIRST_STEP = AT_Q
LAST_TILES_FIRST = STEPS
LAST_STEP = LAST_TILES_FIRST + 2 * (KV - 1)

FLOPS = 2 * H * S * S * HD * 2 + 2 * S * (H * HD) * E


def unit_at(step, lag):
    first = step - lag
    if first % G == 0 and 0 <= first < STEPS:
        return first // G
    return -1


def tile_grupedqueryattention_pb_kernel(tc, q_rot, k_rot, v, wo, out):
    nc = tc.nc
    with ExitStack() as ctx:
        keep = ctx.enter_context(tc.tile_pool(name="keep", bufs=1))
        work = ctx.enter_context(tc.tile_pool(name="work", bufs=2))
        psum_s = ctx.enter_context(tc.psum_pool(name="psum_s", bufs=SCORES_AHEAD + 1))
        psum_e = ctx.enter_context(tc.psum_pool(name="psum_e", bufs=2))
        psum_t = ctx.enter_context(tc.psum_pool(name="psum_t", bufs=1))
        psum_o = ctx.enter_context(tc.psum_pool(name="psum_o", bufs=1))
        ctx.enter_context(tc.manual_schedule())

        q_view = q_rot[0].rearrange("(g h) (p t) d -> g p h (t d)", h=G, t=QT)
        out_view = out[0].rearrange("(p t) n -> t p n", t=QT)
        k_view = k_rot[0].rearrange("g (t p) d -> g p t d", p=P)
        v_view = v[0].rearrange("g (u p e) d -> p (g u) (e d)", u=HALF, e=2)
        wo_view = wo.rearrange("(g u p e) n -> e p (g u) n", g=KV, u=HALF, e=2)

        q_raw = [keep.tile([P, G, QT * HD], BF16, name="q_raw%d" % g) for g in range(KV)]
        k_raw = [keep.tile([P, QT, HD], BF16, name="k_raw%d" % g) for g in range(KV)]
        k_t = [keep.tile([P, S], BF16, name="k_t%d" % g) for g in range(KV)]
        v_raw = keep.tile([P, KV, PACK, HD], BF16, name="v_raw")
        v_grouped = keep.tile([P, KV * HD * PACK], BF16, name="v_grouped", align_bytes=64)
        v_codes = keep.tile([P, KV * HD], U32, name="v_codes", align_bytes=64)
        v_scales = keep.tile([P, KV * HD], U8, name="v_scales", align_bytes=64)
        w_raw = [keep.tile([P, KV, PACK, N_TILE], BF16, name="w_raw%d" % nt) for nt in range(NT)]
        w_codes = keep.tile([P, KV, E], U32, name="w_codes", align_bytes=64)
        w_scales = keep.tile([P, KV, E], U8, name="w_scales", align_bytes=64)
        y_grouped = [
            keep.tile([P, KV * P * PACK], BF16, name="y_grouped%d" % t, align_bytes=64) for t in range(QT)
        ]
        y_codes = [keep.tile([P, KV * P], U32, name="y_codes%d" % t, align_bytes=64) for t in range(QT)]
        y_scales = [keep.tile([P, KV * P], U8, name="y_scales%d" % t, align_bytes=64) for t in range(QT)]
        row_max = keep.tile([P, STEPS], F32, name="row_max")
        exp_bias = keep.tile([P, STEPS], F32, name="exp_bias")
        row_sum = keep.tile([P, STEPS], F32, name="row_sum")
        inv_sum = keep.tile([P, STEPS], F32, name="inv_sum")
        ident_bf = keep.tile([P, P], BF16, name="ident_bf")
        ident_f32 = keep.tile([P, P], F32, name="ident_f32")

        nc.sync.dma_start(out=q_raw[0][:, :, :HD], in_=q_view[0][:, :, :HD])
        nc.sync.dma_start(out=k_raw[0][:], in_=k_view[0])
        nc.sync.dma_start(out=q_raw[0][:, :, HD:], in_=q_view[0][:, :, HD:])
        for g in range(1, KV):
            nc.sync.dma_start(out=k_raw[g][:], in_=k_view[g])
            nc.sync.dma_start(out=q_raw[g][:], in_=q_view[g])
            if g == 1:
                nc.sync.dma_start(
                    out=v_raw[:].rearrange("p g (u e) d -> p (g u) (e d)", u=HALF, e=2), in_=v_view
                )
        for nt in range(NT):
            for e in range(2):
                nc.sync.dma_start(
                    out=w_raw[nt][:, :, e::2, :].rearrange("p g u n -> p (g u) n"),
                    in_=wo_view[e][:, :, nt * N_TILE : (nt + 1) * N_TILE],
                )

        make_identity(nc, ident_bf[:])
        make_identity(nc, ident_f32[:])

        q_t, scores, e_rows, bank_e, e_grouped, e_codes, e_scales = {}, {}, {}, {}, {}, {}, {}
        bank_y, y_rows, bank_yt, w_grouped, acc, last_acc = {}, {}, {}, {}, {}, {}

        def transposed_words(bank, rows_bf16):
            words = rows_bf16.bitcast(F32)
            for u in range(HALF):
                nc.tensor.transpose(bank[:, u, :], words[:, u * P : (u + 1) * P], ident_f32[:])

        def score_matmul(n):
            unit, h = n // G, n % G
            scores[n] = psum_s.tile([P, S], F32, name="scores", tag="s")
            nc.tensor.matmul(
                out=scores[n][:],
                lhsT=q_t[unit][:, h * P : (h + 1) * P],
                rhs=k_t[unit % KV][:],
                start=True,
                stop=True,
            )

        def score_max(n):
            nc.vector.tensor_reduce(out=row_max[:, n : n + 1], in_=scores[n][:], axis=AXIS_X, op=MAX)

        def score_bias(n):
            nc.scalar.mul(out=exp_bias[:, n : n + 1], in_=row_max[:, n : n + 1], mul=-SCALE)

        def exponentials(n):
            e_rows[n] = work.tile([P, S], BF16, name="e_rows", bufs=3)
            nc.scalar.activation(
                out=e_rows[n][:],
                in_=scores[n][:],
                func=EXP,
                bias=exp_bias[:, n : n + 1],
                scale=SCALE,
                accum_out=row_sum[:, n : n + 1],
            )

        def e_transpose(n):
            bank_e[n] = psum_e.tile([P, HALF, P], F32, name="bank_e")
            transposed_words(bank_e[n][:], e_rows[n][:])

        def e_copy(n):
            unit, h = n // G, n % G
            if h == 0:
                e_grouped[unit] = work.tile([P, G * P * PACK], BF16, name="e_grouped", align_bytes=64)
            e_words = e_grouped[unit][:].bitcast(F32).rearrange("p (h q u) -> p h q u", h=G, u=HALF)
            nc.scalar.copy(out=e_words[:, h], in_=bank_e[n][:].rearrange("p u q -> p q u"))

        def key_transpose(g):
            bank_k = psum_o.tile([P, S], BF16, name="bank_k", tag="o")
            for t in range(QT):
                nc.tensor.transpose(bank_k[:, t * P : (t + 1) * P], k_raw[g][:, t, :], ident_bf[:])
            nc.scalar.copy(out=k_t[g][:], in_=bank_k[:])

        def query_transpose(unit):
            qt, g = unit // KV, unit % KV
            bank_q = psum_t.tile([P, G * P], BF16, name="bank_q", tag="t")
            for h in range(G):
                nc.tensor.transpose(
                    bank_q[:, h * P : (h + 1) * P], q_raw[g][:, h, qt * HD : (qt + 1) * HD], ident_bf[:]
                )
            q_t[unit] = work.tile([P, G * P], BF16, name="q_t")
            nc.scalar.copy(out=q_t[unit][:], in_=bank_q[:])

        def e_quantise(unit):
            e_codes[unit] = work.tile([P, G * P], U32, name="e_codes", align_bytes=64)
            e_scales[unit] = work.tile([P, G * P], U8, name="e_scales", align_bytes=64)
            nc.vector.quantize_mx(
                out=e_codes[unit][:].bitcast(FP8X4), scales=e_scales[unit][:], in_=e_grouped[unit][:]
            )
            heads = slice(unit * G, (unit + 1) * G)
            nc.vector.reciprocal(out=inv_sum[:, heads], in_=row_sum[:, heads])

        def e_times_v(unit):
            g = unit % KV
            bank_y[unit] = psum_t.tile([P, G * HD], F32, name="bank_y", tag="t")
            for h in range(G):
                rows = slice(h * P, (h + 1) * P)
                nc.tensor.matmul_mx(
                    out=bank_y[unit][:, h * HD : (h + 1) * HD],
                    lhsT=e_codes[unit][:, rows].bitcast(FP8X4),
                    lhsT_scale=e_scales[unit][:, rows],
                    rhs=v_codes[:, g * HD : (g + 1) * HD].bitcast(FP8X4),
                    rhs_scale=v_scales[:, g * HD : (g + 1) * HD],
                    start=True,
                    stop=True,
                )
            y_rows[unit] = work.tile([P, G * HD], BF16, name="y_rows")
            for h in range(G):
                nc.scalar.activation(
                    out=y_rows[unit][:, h * HD : (h + 1) * HD],
                    in_=bank_y[unit][:, h * HD : (h + 1) * HD],
                    func=COPY,
                    scale=inv_sum[:, unit * G + h : unit * G + h + 1],
                )

        def y_transpose(unit):
            bank_yt[unit] = psum_t.tile([P, HALF, P], F32, name="bank_yt", tag="t")
            transposed_words(bank_yt[unit][:], y_rows[unit][:])

        def y_copy(unit):
            qt, g = unit // KV, unit % KV
            y_words = y_grouped[qt][:].bitcast(F32).rearrange("p (g q u) -> p g q u", g=KV, u=HALF)
            nc.scalar.copy(out=y_words[:, g], in_=bank_yt[unit][:].rearrange("p u q -> p q u"))

        def y_quantise(unit):
            qt, g = unit // KV, unit % KV
            nc.vector.quantize_mx(
                out=y_codes[qt][:, g * P : (g + 1) * P].bitcast(FP8X4),
                scales=y_scales[qt][:, g * P : (g + 1) * P],
                in_=y_grouped[qt][:, g * P * PACK : (g + 1) * P * PACK],
            )

        def prepare_v():
            nc.vector.tensor_copy(
                out=v_grouped[:].rearrange("p (g d t) -> p g d t", g=KV, t=PACK),
                in_=v_raw[:].rearrange("p g t d -> p g d t"),
            )
            nc.vector.quantize_mx(out=v_codes[:].bitcast(FP8X4), scales=v_scales[:], in_=v_grouped[:])

        def wo_regroup(chunk, half):
            nt, g = chunk // KV, chunk % KV
            if half == 0:
                w_grouped[chunk] = work.tile([P, N_TILE * PACK], BF16, name="w_grouped", align_bytes=64)
            cols = slice(half * (N_TILE // 2), (half + 1) * (N_TILE // 2))
            nc.vector.tensor_copy(
                out=w_grouped[chunk][:].rearrange("p (n t) -> p n t", t=PACK)[:, cols].rearrange(
                    "p (c i) t -> p c t i", i=4
                ),
                in_=w_raw[nt][:, g, :, cols].rearrange("p t (c i) -> p c t i", i=4),
            )

        def wo_quantise(chunk):
            nt, g = chunk // KV, chunk % KV
            cols = slice(nt * N_TILE, (nt + 1) * N_TILE)
            nc.vector.quantize_mx(
                out=w_codes[:, g, cols].bitcast(FP8X4), scales=w_scales[:, g, cols], in_=w_grouped[chunk][:]
            )

        def projection_pass(bank, qt, nt, g):
            rows = slice(g * P, (g + 1) * P)
            cols = slice(nt * N_TILE, (nt + 1) * N_TILE)
            nc.tensor.matmul_mx(
                out=bank[:],
                lhsT=y_codes[qt][:, rows].bitcast(FP8X4),
                lhsT_scale=y_scales[qt][:, rows],
                rhs=w_codes[:, g, cols].bitcast(FP8X4),
                rhs_scale=w_scales[:, g, cols],
                start=(g == 0),
                stop=(g == KV - 1),
            )

        def store_tile(bank, qt, nt, on_vector):
            result = work.tile([P, N_TILE], F32, name="result", bufs=4)
            if on_vector:
                nc.vector.tensor_copy(out=result[:], in_=bank[:])
            else:
                nc.scalar.copy(out=result[:], in_=bank[:])
            nc.sync.dma_start(out=out_view[qt][:, nt * N_TILE : (nt + 1) * N_TILE], in_=result[:])

        units_ready = 0
        chunks_ready = 0
        issued = []
        stored = 0
        for step in range(FIRST_STEP, LAST_STEP + 1):
            if 0 <= step + SCORES_AHEAD < STEPS:
                score_matmul(step + SCORES_AHEAD)
            if 0 <= step - 1 < STEPS:
                e_transpose(step - 1)
            if 0 <= step + MAX_AHEAD < STEPS:
                score_max(step + MAX_AHEAD)
            if 0 <= step < STEPS:
                exponentials(step)
            if 0 <= step + BIAS_AHEAD < STEPS:
                score_bias(step + BIAS_AHEAD)
            if 0 <= step - 1 < STEPS:
                e_copy(step - 1)

            unit = unit_at(step, AT_Y_COPY)
            if unit >= 0:
                y_copy(unit)
            unit = unit_at(step, AT_Q)
            if unit >= 0:
                if unit < KV:
                    key_transpose(unit)
                query_transpose(unit)
            unit = unit_at(step, AT_E_QUANT)
            if unit >= 0:
                e_quantise(unit)
            unit = unit_at(step, AT_PV)
            if unit >= 0:
                e_times_v(unit)
            unit = unit_at(step, AT_Y_TRANSPOSE)
            if unit >= 0:
                y_transpose(unit)
            unit = unit_at(step, AT_Y_QUANT)
            if unit >= 0:
                y_quantise(unit)
                units_ready = unit + 1
            if step == 1:
                prepare_v()

            since = step - WO_FIRST
            if 0 <= since < CHUNKS * WO_EVERY:
                if since % WO_EVERY < 2:
                    wo_regroup(since // WO_EVERY, since % WO_EVERY)
                else:
                    wo_quantise(since // WO_EVERY)
                    chunks_ready = since // WO_EVERY + 1

            if stored < len(issued):
                qt, nt = issued[stored]
                store_tile(acc[(qt, nt)], qt, nt, chunks_ready == CHUNKS)
                stored += 1
            if step % 2 == 0:
                ready = [
                    (qt, nt)
                    for qt in range(QT - 1)
                    for nt in range(NT)
                    if (qt, nt) not in issued and units_ready >= (qt + 1) * KV and chunks_ready >= (nt + 1) * KV
                ]
                if ready:
                    qt, nt = ready[0]
                    acc[(qt, nt)] = psum_o.tile([P, N_TILE], F32, name="acc", tag="o")
                    for g in range(KV):
                        projection_pass(acc[(qt, nt)], qt, nt, g)
                    issued.append((qt, nt))
            since = step - LAST_TILES_FIRST
            if since >= 0 and since % 2 == 0:
                g = since // 2
                for nt in range(NT):
                    if g == 0:
                        last_acc[nt] = psum_s.tile([P, N_TILE], F32, name="last_acc", tag="s")
                    projection_pass(last_acc[nt], QT - 1, nt, g)
        assert len(issued) == (QT - 1) * NT and stored == len(issued)
        for nt in range(NT):
            store_tile(last_acc[nt], QT - 1, nt, nt % 2 == 0)
